import numpy as np
import ml_dtypes


def mxq(x, axis, fmt="e4m3"):
    dtype, down = {"e4m3": (ml_dtypes.float8_e4m3fn, 7), "e5m2": (ml_dtypes.float8_e5m2, 14)}[fmt]
    v = np.moveaxis(np.asarray(x, np.float32).astype(ml_dtypes.bfloat16).astype(np.float64), axis, -1)
    blocks = v.reshape(v.shape[:-1] + (-1, 32))
    amax = np.abs(blocks).max(-1, keepdims=True)
    byte = np.maximum(np.where(amax > 0, np.frexp(amax)[1] - 1 + 127, 0) - down, 1)
    scale = np.exp2(byte - 127.0)
    codes = (blocks / scale).astype(np.float32).astype(dtype).astype(np.float64)
    return np.moveaxis((codes * scale).reshape(v.shape), -1, axis)


WIDE = False


def mx_kscale(k):
    if not WIDE:
        return np.ones(k)
    levels = np.array([10, -10, 5, -5, 0])
    a = np.random.permutation(np.resize(levels, k // 512 * 4)).reshape(k // 512, 4)
    idx = np.arange(k)
    return np.exp2(a[idx // 512, idx % 128 // 32])


BF16 = ml_dtypes.bfloat16


def bf(x):
    return np.asarray(x, np.float32).astype(BF16)


def f64(x):
    return np.asarray(x).astype(np.float64)


E2M1 = np.array([0.0, 0.5, 1.0, 1.5, 2.0, 3.0, 4.0, 6.0, -0.0, -0.5, -1.0, -1.5, -2.0, -3.0, -4.0, -6.0])


def pack_weight(w, fmt):
    k, n = w.shape
    w = f64(bf(w)).reshape(k // 32, 32, n)
    amax = np.abs(w).max(1)
    if fmt == "e4m3":
        byte = np.frexp(amax)[1] - 1 + 127 - 7
    else:
        mant, ex = np.frexp(amax / 6.0)
        byte = np.where(mant > 0.5, ex, ex - 1) + 127
    byte = np.clip(np.where(amax > 0, byte, 1), 1, 254)
    scaled = (w * np.exp2(127.0 - byte)[:, None, :]).reshape(k, n).astype(np.float32)
    by_word = np.ascontiguousarray(scaled.reshape(k // 512, 128, 4, n).transpose(0, 1, 3, 2))
    if fmt == "e4m3":
        words = by_word.astype(ml_dtypes.float8_e4m3fn).view(np.uint8)
    else:
        c = by_word.astype(ml_dtypes.float4_e2m1fn).view(np.uint8) & 0xF
        words = c[..., 0::2] | (c[..., 1::2] << 4)
    return np.ascontiguousarray(words), np.ascontiguousarray(byte.astype(np.uint8).reshape(k // 512, 16, n))


def unpack_weight(words, scales, fmt):
    g, p, n, _ = words.shape
    if fmt == "e4m3":
        vals = np.ascontiguousarray(words).view(ml_dtypes.float8_e4m3fn).astype(np.float64)
    else:
        nib = np.empty((g, p, n, 4), np.uint8)
        nib[..., 0::2] = words & 0xF
        nib[..., 1::2] = words >> 4
        vals = E2M1[nib]
    vals = vals * np.repeat(np.exp2(scales.astype(np.float64) - 127.0), 8, axis=1)[..., None]
    return vals.transpose(0, 1, 3, 2).reshape(g * 512, n)


B, S, D, E = 1, 128, 2048, 2048
INV_SQRT2 = 0.7071067811865476
FMT = "e4m3"


def dwt_haar(x):
    e = x[..., 0::2]
    o = x[..., 1::2]
    return (e + o) * INV_SQRT2, (o - e) * INV_SQRT2


def idwt_haar(L, H):
    a = (L - H) * INV_SQRT2
    b = (L + H) * INV_SQRT2
    return np.stack([a, b], axis=-1).reshape(*L.shape[:-1], -1)


def softmax(v):
    p = np.exp(v - v.max(-1, keepdims=True))
    return p / p.sum(-1, keepdims=True)


def setup_inputs():
    s = mx_kscale(D)
    x = bf(np.random.standard_normal((B, S, D)) * s)
    W_q_words, W_q_scales = pack_weight(np.ascontiguousarray((np.random.standard_normal((E, D)) * 1.5 / np.sqrt(D) / s).T), FMT)
    b_q = bf(np.random.standard_normal(E) * 0.5)
    W_k_words, W_k_scales = pack_weight(np.ascontiguousarray((np.random.standard_normal((E, D)) * 1.5 / np.sqrt(D) / s).T), FMT)
    b_k = bf(np.random.standard_normal(E) * 0.5)
    W_v_words, W_v_scales = pack_weight(np.ascontiguousarray((np.random.standard_normal((E, D)) * 2.0 / np.sqrt(D) / s).T), FMT)
    b_v = bf(np.random.standard_normal(E) * 0.5)
    return {"x": x,
            "W_q_words": W_q_words, "W_q_scales": W_q_scales,
            "b_q": b_q,
            "W_k_words": W_k_words, "W_k_scales": W_k_scales,
            "b_k": b_k,
            "W_v_words": W_v_words, "W_v_scales": W_v_scales,
            "b_v": b_v}


def reference(x, W_q_words, W_q_scales, b_q, W_k_words, W_k_scales, b_k, W_v_words, W_v_scales, b_v):
    nb, ns = x.shape[0], x.shape[1]
    xq = mxq(f64(x), 2, "e4m3")
    q = (xq @ unpack_weight(W_q_words, W_q_scales, FMT)) + f64(b_q)
    k = (xq @ unpack_weight(W_k_words, W_k_scales, FMT)) + f64(b_k)
    v = (xq @ unpack_weight(W_v_words, W_v_scales, FMT)) + f64(b_v)
    q_L, q_H = dwt_haar(q)
    k_L, k_H = dwt_haar(k)
    v_L, v_H = dwt_haar(v)
    L = softmax(q_L + k_L)
    H = softmax(q_H + k_H)
    L_out = softmax(L + v_L)
    H_out = softmax(H + v_H)
    out = idwt_haar(L_out, H_out)
    return out.reshape(nb, ns, -1)

@@ -1,0 +1,240 @@
+from contextlib import ExitStack
+
+import concourse.masks as masks
+import concourse.mybir as mybir
+
+FLOPS = 3 * 2 * 128 * 2048 * 2048
+
+F32 = mybir.dt.float32
+BF16 = mybir.dt.bfloat16
+U8 = mybir.dt.uint8
+U32 = mybir.dt.uint32
+I32 = mybir.dt.int32
+FP8X4 = mybir.dt.float8_e4m3fn_x4
+ALU = mybir.AluOpType
+ACT = mybir.ActivationFunctionType
+AX = mybir.AxisListType
+
+P = 128
+D = 2048
+G = 4
+NCH = 4
+CW = 512
+HW = 256
+C = 0.7071067811865476
+
+
+def tile_waveletmultiheadattention_w_kernel(
+    tc, x, wq_words, wq_scales, b_q, wk_words, wk_scales, b_k, wv_words, wv_scales, b_v, out
+):
+    nc = tc.nc
+    with ExitStack() as ctx:
+        keep = ctx.enter_context(tc.tile_pool(name="keep", bufs=1))
+        psum = ctx.enter_context(tc.psum_pool(name="psum", bufs=1))
+        ctx.enter_context(tc.manual_schedule())
+
+        zero1 = keep.tile([P, 1], F32, name="zero1")
+        warm = keep.tile([P, 1], F32, name="warm")
+        nc.vector.memset(zero1[:], 0.0)
+        nc.scalar.activation(out=warm[:], in_=zero1[:], func=ACT.Exp)
+
+        planes = [keep.tile([P, D], U8, name="planes%d" % w, align_bytes=64) for w in range(3)]
+        for w in range(3):
+            nc.vector.memset(planes[w][:].bitcast(I32), 0)
+        rows = keep.tile([P, 2, D], BF16, name="rows")
+        nc.vector.memset(rows[:].rearrange("p w n -> p (w n)").bitcast(I32), 0)
+
+        ident = keep.tile([P, P], F32, name="ident")
+        masks.make_identity(nc, ident[:])
+        pos = keep.tile([P, P], BF16, name="pos")
+        neg = keep.tile([P, P], BF16, name="neg")
+        nc.gpsimd.memset(pos[:], 1.0)
+        nc.gpsimd.memset(neg[:], -1.0)
+
+        x_sb = keep.tile([P, D], BF16, name="x_sb")
+        nc.sync.dma_start(out=x_sb[:], in_=x.flatten_outer_dims())
+        nc.scalar.dma_start(out=rows[0:1, 0, :], in_=b_q.unsqueeze(0))
+        nc.scalar.dma_start(out=rows[1:2, 0, :], in_=b_k.unsqueeze(0))
+        nc.scalar.dma_start(out=rows[0:1, 1, :], in_=b_v.unsqueeze(0))
+        for w, sc in enumerate((wq_scales, wk_scales, wv_scales)):
+            for q in range(4):
+                nc.sync.dma_start(
+                    out=planes[w][32 * q : 32 * q + 16, :].bitcast(I32),
+                    in_=sc[:, 4 * q : 4 * q + 4, :].bitcast(I32),
+                )
+        wq = [keep.tile([P, D], U32, name="wq%d" % g, align_bytes=64) for g in range(G)]
+        for g in range(G):
+            nc.sync.dma_start(
+                out=wq[g][:].bitcast(I32),
+                in_=wq_words[g].rearrange("p n t -> p (n t)").bitcast(I32),
+            )
+        wk = [keep.tile([P, G, CW], U32, name="wk%d" % c, align_bytes=64) for c in range(NCH)]
+        wv = [keep.tile([P, G, CW], U32, name="wv%d" % c, align_bytes=64) for c in range(NCH)]
+        for tiles, words in ((wk, wk_words), (wv, wv_words)):
+            view = words.rearrange("g p n t -> p g (n t)").bitcast(I32)
+            for c in range(NCH):
+                nc.sync.dma_start(out=tiles[c][:].bitcast(I32), in_=view[:, :, c * CW : (c + 1) * CW])
+
+        x32 = x_sb[:].bitcast(F32)
+        grouped = keep.tile([P, D], BF16, name="grouped", align_bytes=64)
+        g32 = grouped[:].bitcast(F32).rearrange("p (g r u) -> p g r u", g=G, u=2)
+        xt = [psum.tile([P, 2, 2, P], F32, name="xt%d" % b, tag="b%d" % (4 + b)) for b in range(2)]
+        for g in range(G):
+            for u in range(2):
+                nc.tensor.transpose(
+                    out=xt[g // 2][:, g % 2, u, :],
+                    in_=x32[:, 256 * g + u : 256 * (g + 1) : 2],
+                    identity=ident[:],
+                )
+        nc.vector.tensor_copy(out=g32[:, 0:2], in_=xt[0][:].rearrange("p g u r -> p g r u"))
+        nc.scalar.copy(out=g32[:, 2:4], in_=xt[1][:].rearrange("p g u r -> p g r u"))
+        xc = keep.tile([P, G * P], U32, name="xc", align_bytes=64)
+        xs = keep.tile([P, G * P], U8, name="xs", align_bytes=64)
+        nc.vector.quantize_mx(out=xc[:].bitcast(FP8X4), scales=xs[:], in_=grouped[:])
+
+        cb = [[keep.tile([P, 2, HW], F32, name="cb%d_%d" % (w, c)) for c in range(NCH)] for w in range(2)]
+        bias_banks = (6, 7, 4, 5)
+        for w in range(2):
+            rv = rows[:, w, :].rearrange("p (c j t) -> p c j t", c=NCH, t=2)
+            for c in range(NCH):
+                bb = psum.tile([P, 2, HW], F32, name="bb%d_%d" % (w, c), tag="b%d" % bias_banks[c])
+                nc.tensor.matmul(out=bb[:, 0, :], lhsT=pos[:], rhs=rv[:, c, :, 0], start=True, stop=False)
+                nc.tensor.matmul(out=bb[:, 0, :], lhsT=pos[:], rhs=rv[:, c, :, 1], start=False, stop=True)
+                nc.tensor.matmul(out=bb[:, 1, :], lhsT=pos[:], rhs=rv[:, c, :, 1], start=True, stop=False)
+                nc.tensor.matmul(out=bb[:, 1, :], lhsT=neg[:], rhs=rv[:, c, :, 0], start=False, stop=True)
+                nc.scalar.activation(out=cb[w][c][:], in_=bb[:], func=ACT.Copy, scale=C)
+
+        def mx_pass(bank, g, words, plane, cols, start, stop):
+            nc.tensor.matmul_mx(
+                out=bank[:],
+                lhsT=xc[:, g * P : (g + 1) * P].bitcast(FP8X4),
+                lhsT_scale=xs[:, g * P : (g + 1) * P],
+                rhs=words.bitcast(FP8X4),
+                rhs_scale=plane[4 * g : P, cols],
+                start=start,
+                stop=stop,
+            )
+
+        def haar(bank, addend, t):
+            pairs = bank[:].rearrange("p (j t) -> p j t", t=2)
+            even = pairs[:, :, 0]
+            odd = pairs[:, :, 1]
+            nc.vector.scalar_tensor_tensor(
+                out=t[:], in0=odd.unsqueeze(1).to_broadcast([P, 2, HW]), scalar=C, in1=addend[:],
+                op0=ALU.mult, op1=ALU.add,
+            )
+            nc.vector.scalar_tensor_tensor(
+                out=t[:, 0, :], in0=even, scalar=C, in1=t[:, 0, :], op0=ALU.mult, op1=ALU.add
+            )
+            nc.vector.scalar_tensor_tensor(
+                out=t[:, 1, :], in0=even, scalar=-C, in1=t[:, 1, :], op0=ALU.mult, op1=ALU.add
+            )
+
+        def shift_and_exp(t, nm, ss, e_low, e_high, c):
+            nc.vector.tensor_reduce(out=nm[:, :, c], in_=t[:], axis=AX.X, op=ALU.max, negate=True)
+            nc.scalar.activation(
+                out=e_low, in_=t[:, 0, :], func=ACT.Exp, bias=nm[:, 0, c : c + 1], scale=1.0,
+                accum_out=ss[:, 0, c : c + 1],
+            )
+            nc.scalar.activation(
+                out=e_high, in_=t[:, 1, :], func=ACT.Exp, bias=nm[:, 1, c : c + 1], scale=1.0,
+                accum_out=ss[:, 1, c : c + 1],
+            )
+
+        def chunk_factors(nm, tag):
+            gm = keep.tile([P, 2], F32, name="gm" + tag)
+            f = keep.tile([P, 2, NCH], F32, name="f" + tag)
+            nc.vector.tensor_reduce(out=gm[:], in_=nm[:], axis=AX.X, op=ALU.min)
+            for h in range(2):
+                nc.scalar.activation(
+                    out=f[:, h, :], in_=nm[:, h, :], func=ACT.Exp, bias=gm[:, h : h + 1], scale=-1.0
+                )
+            return f
+
+        def chunk_scales(f, ss, post, tag):
+            fs = keep.tile([P, 2, NCH], F32, name="fs" + tag)
+            tot = keep.tile([P, 2], F32, name="tot" + tag)
+            rec = keep.tile([P, 2], F32, name="rec" + tag)
+            sc = keep.tile([P, 2, NCH], F32, name="sc" + tag)
+            nc.vector.tensor_tensor(out=fs[:], in0=f[:], in1=ss[:], op=ALU.mult)
+            nc.vector.tensor_reduce(out=tot[:], in_=fs[:], axis=AX.X, op=ALU.add)
+            nc.vector.reciprocal(out=rec[:], in_=tot[:])
+            nc.vector.scalar_tensor_tensor(
+                out=sc[:], in0=f[:], scalar=post, in1=rec[:].unsqueeze(2).to_broadcast([P, 2, NCH]),
+                op0=ALU.mult, op1=ALU.mult,
+            )
+            return sc
+
+        qk = [psum.tile([P, CW], F32, name="qk%d" % c, tag="b%d" % c) for c in range(NCH)]
+        for g in range(G):
+            for c in range(NCH):
+                cols = slice(c * CW, (c + 1) * CW)
+                mx_pass(qk[c], g, wq[g][:, cols], planes[0], cols, g == 0, False)
+        nm1 = keep.tile([P, 2, NCH], F32, name="nm1")
+        ss1 = keep.tile([P, 2, NCH], F32, name="ss1")
+        t1 = [keep.tile([P, 2, HW], F32, name="t1_%d" % c) for c in range(NCH)]
+        e1 = [keep.tile([P, 2, HW], F32, name="e1_%d" % c) for c in range(NCH)]
+        for c in range(NCH):
+            cols = slice(c * CW, (c + 1) * CW)
+            for g in range(G):
+                mx_pass(qk[c], g, wk[c][:, g, :], planes[1], cols, False, g == G - 1)
+            haar(qk[c], cb[0][c], t1[c])
+            shift_and_exp(t1[c], nm1, ss1, e1[c][:, 0, :], e1[c][:, 1, :], c)
+
+        nm2 = keep.tile([P, 2, NCH], F32, name="nm2")
+        ss2 = keep.tile([P, 2, NCH], F32, name="ss2")
+        t2 = [keep.tile([P, 2, HW], F32, name="t2_%d" % c) for c in range(NCH)]
+        e2 = [keep.tile([P, 3, HW], F32, name="e2_%d" % c) for c in range(NCH)]
+        lb = [keep.tile([P, 2, HW], F32, name="lb%d" % c) for c in range(NCH)]
+        f1 = chunk_factors(nm1, "1")
+        sc1 = None
+        for c in range(NCH):
+            cols = slice(c * CW, (c + 1) * CW)
+            vb = psum.tile([P, CW], F32, name="v%d" % c, tag="b%d" % (4 + c))
+            for g in range(G):
+                mx_pass(vb, g, wv[c][:, g, :], planes[2], cols, g == 0, g == G - 1)
+            if c == 0:
+                haar(vb, cb[1][0], t2[0])
+                sc1 = chunk_scales(f1, ss1, 1.0, "1")
+                for cc in (2, 3):
+                    for h in range(2):
+                        nc.scalar.activation(
+                            out=e1[cc][:, h, :], in_=e1[cc][:, h, :], func=ACT.Copy, scale=sc1[:, h, cc : cc + 1]
+                        )
+                    nc.gpsimd.tensor_tensor(out=lb[cc][:], in0=e1[cc][:], in1=cb[1][cc][:], op=ALU.add)
+                for h in range(2):
+                    nc.vector.scalar_tensor_tensor(
+                        out=t2[0][:, h, :], in0=e1[0][:, h, :], scalar=sc1[:, h, 0:1], in1=t2[0][:, h, :],
+                        op0=ALU.mult, op1=ALU.add,
+                    )
+            else:
+                if c == 1:
+                    for h in range(2):
+                        nc.vector.scalar_tensor_tensor(
+                            out=lb[1][:, h, :], in0=e1[1][:, h, :], scalar=sc1[:, h, 1:2], in1=cb[1][1][:, h, :],
+                            op0=ALU.mult, op1=ALU.add,
+                        )
+                haar(vb, lb[c], t2[c])
+            shift_and_exp(t2[c], nm2, ss2, e2[c][:, 0, :], e2[c][:, 2, :], c)
+            nc.gpsimd.tensor_scalar(
+                out=e2[c][:, 1, :], in0=e2[c][:, 2, :], scalar1=-1.0, scalar2=0.0, op0=ALU.mult, op1=ALU.add
+            )
+        sc2 = chunk_scales(chunk_factors(nm2, "2"), ss2, C, "2")
+        out2d = out.flatten_outer_dims()
+        for c in range(NCH):
+            low = keep.tile([P, HW], F32, name="low%d" % c)
+            res = keep.tile([P, CW], F32, name="res%d" % c)
+            if c == 0:
+                nc.vector.tensor_scalar(
+                    out=low[:], in0=e2[c][:, 0, :], scalar1=sc2[:, 0, c : c + 1], scalar2=None, op0=ALU.mult
+                )
+            else:
+                nc.scalar.activation(out=low[:], in_=e2[c][:, 0, :], func=ACT.Copy, scale=sc2[:, 0, c : c + 1])
+            nc.vector.scalar_tensor_tensor(
+                out=res[:].rearrange("p (j t) -> p j t", t=2),
+                in0=e2[c][:, 1:3, :].rearrange("p t j -> p j t"),
+                scalar=sc2[:, 1, c : c + 1],
+                in1=low[:].unsqueeze(2).to_broadcast([P, HW, 2]),
+                op0=ALU.mult, op1=ALU.add,
+            )
+            nc.sync.dma_start(out=out2d[:, c * CW : (c + 1) * CW], in_=res[:])

@@ -23,6 +23,20 @@ CW = 512
 HW = 256
 C = 0.7071067811865476
 
+SPLIT_K = (3,)
+VCH = ((0, 512), (512, 512), (1024, 512), (1536, 512))
+NV = len(VCH)
+VBANK = (4, 5, 6, 7)
+SPLIT_V = (0, 3)
+POST = (0, 1)
+POOL_ORDER = (2, 3, 0, 1)
+ACT_LS_ORDER = (2, 3, 0, 1)
+EXP_ORDER = (0, 2, 1, 3)
+COMB_AFTER_ODD = True
+NEG_ON_ACT = (3,)
+VSCALES_LATE = True
+DVE_LB = ()
+
 
 def tile_waveletmultiheadattention_w_kernel(
     tc, x, wq_words, wq_scales, b_q, wk_words, wk_scales, b_k, wv_words, wv_scales, b_v, out
@@ -56,12 +70,17 @@ def tile_waveletmultiheadattention_w_kernel(
         nc.scalar.dma_start(out=rows[0:1, 0, :], in_=b_q.unsqueeze(0))
         nc.scalar.dma_start(out=rows[1:2, 0, :], in_=b_k.unsqueeze(0))
         nc.scalar.dma_start(out=rows[0:1, 1, :], in_=b_v.unsqueeze(0))
-        for w, sc in enumerate((wq_scales, wk_scales, wv_scales)):
+        def load_scales(w, sc):
             for q in range(4):
                 nc.sync.dma_start(
                     out=planes[w][32 * q : 32 * q + 16, :].bitcast(I32),
                     in_=sc[:, 4 * q : 4 * q + 4, :].bitcast(I32),
                 )
+
+        load_scales(0, wq_scales)
+        load_scales(1, wk_scales)
+        if not VSCALES_LATE:
+            load_scales(2, wv_scales)
         wq = [keep.tile([P, D], U32, name="wq%d" % g, align_bytes=64) for g in range(G)]
         for g in range(G):
             nc.sync.dma_start(
@@ -69,11 +88,19 @@ def tile_waveletmultiheadattention_w_kernel(
                 in_=wq_words[g].rearrange("p n t -> p (n t)").bitcast(I32),
             )
         wk = [keep.tile([P, G, CW], U32, name="wk%d" % c, align_bytes=64) for c in range(NCH)]
-        wv = [keep.tile([P, G, CW], U32, name="wv%d" % c, align_bytes=64) for c in range(NCH)]
-        for tiles, words in ((wk, wk_words), (wv, wv_words)):
+        wv = [keep.tile([P, G, VCH[i][1]], U32, name="wv%d" % i, align_bytes=64) for i in range(NV)]
+        KCH = tuple((c * CW, CW) for c in range(NCH))
+        for tiles, words, split, chunks in ((wk, wk_words, SPLIT_K, KCH), (wv, wv_words, SPLIT_V, VCH)):
             view = words.rearrange("g p n t -> p g (n t)").bitcast(I32)
-            for c in range(NCH):
-                nc.sync.dma_start(out=tiles[c][:].bitcast(I32), in_=view[:, :, c * CW : (c + 1) * CW])
+            if VSCALES_LATE and tiles is wv:
+                load_scales(2, wv_scales)
+            for c, (c0, cw) in enumerate(chunks):
+                cols = slice(c0, c0 + cw)
+                if c in split:
+                    nc.sync.dma_start(out=tiles[c][:, 0:3, :].bitcast(I32), in_=view[:, 0:3, cols])
+                    nc.sync.dma_start(out=tiles[c][:, 3:4, :].bitcast(I32), in_=view[:, 3:4, cols])
+                else:
+                    nc.sync.dma_start(out=tiles[c][:].bitcast(I32), in_=view[:, :, cols])
 
         x32 = x_sb[:].bitcast(F32)
         grouped = keep.tile([P, D], BF16, name="grouped", align_bytes=64)
@@ -115,23 +142,25 @@ def tile_waveletmultiheadattention_w_kernel(
                 stop=stop,
             )
 
-        def haar(bank, addend, t):
-            pairs = bank[:].rearrange("p (j t) -> p j t", t=2)
-            even = pairs[:, :, 0]
-            odd = pairs[:, :, 1]
-            nc.vector.scalar_tensor_tensor(
-                out=t[:], in0=odd.unsqueeze(1).to_broadcast([P, 2, HW]), scalar=C, in1=addend[:],
-                op0=ALU.mult, op1=ALU.add,
-            )
-            nc.vector.scalar_tensor_tensor(
-                out=t[:, 0, :], in0=even, scalar=C, in1=t[:, 0, :], op0=ALU.mult, op1=ALU.add
-            )
-            nc.vector.scalar_tensor_tensor(
-                out=t[:, 1, :], in0=even, scalar=-C, in1=t[:, 1, :], op0=ALU.mult, op1=ALU.add
-            )
+        def haar_odd(bank, addend, t):
+            odd = bank[:].rearrange("p (j t) -> p j t", t=2)[:, :, 1]
+            for h in range(2):
+                nc.vector.scalar_tensor_tensor(
+                    out=t[:, h, :], in0=odd, scalar=C, in1=addend[:, h, :], op0=ALU.mult, op1=ALU.add
+                )
 
-        def shift_and_exp(t, nm, ss, e_low, e_high, c):
-            nc.vector.tensor_reduce(out=nm[:, :, c], in_=t[:], axis=AX.X, op=ALU.max, negate=True)
+        def haar_even(bank, t):
+            even = bank[:].rearrange("p (j t) -> p j t", t=2)[:, :, 0]
+            for h in range(2):
+                nc.vector.scalar_tensor_tensor(
+                    out=t[:, h, :], in0=even, scalar=(C, -C)[h], in1=t[:, h, :], op0=ALU.mult, op1=ALU.add
+                )
+
+        def maxes(t, nm, c):
+            for h in range(2):
+                nc.vector.tensor_reduce(out=nm[:, h, c : c + 1], in_=t[:, h, :], axis=AX.X, op=ALU.max, negate=True)
+
+        def exps(t, nm, ss, e_low, e_high, c):
             nc.scalar.activation(
                 out=e_low, in_=t[:, 0, :], func=ACT.Exp, bias=nm[:, 0, c : c + 1], scale=1.0,
                 accum_out=ss[:, 0, c : c + 1],
@@ -141,9 +170,9 @@ def tile_waveletmultiheadattention_w_kernel(
                 accum_out=ss[:, 1, c : c + 1],
             )
 
-        def chunk_factors(nm, tag):
+        def chunk_factors(nm, tag, n):
             gm = keep.tile([P, 2], F32, name="gm" + tag)
-            f = keep.tile([P, 2, NCH], F32, name="f" + tag)
+            f = keep.tile([P, 2, n], F32, name="f" + tag)
             nc.vector.tensor_reduce(out=gm[:], in_=nm[:], axis=AX.X, op=ALU.min)
             for h in range(2):
                 nc.scalar.activation(
@@ -151,16 +180,16 @@ def tile_waveletmultiheadattention_w_kernel(
                 )
             return f
 
-        def chunk_scales(f, ss, post, tag):
-            fs = keep.tile([P, 2, NCH], F32, name="fs" + tag)
+        def chunk_scales(f, ss, post, tag, n):
+            fs = keep.tile([P, 2, n], F32, name="fs" + tag)
             tot = keep.tile([P, 2], F32, name="tot" + tag)
             rec = keep.tile([P, 2], F32, name="rec" + tag)
-            sc = keep.tile([P, 2, NCH], F32, name="sc" + tag)
+            sc = keep.tile([P, 2, n], F32, name="sc" + tag)
             nc.vector.tensor_tensor(out=fs[:], in0=f[:], in1=ss[:], op=ALU.mult)
             nc.vector.tensor_reduce(out=tot[:], in_=fs[:], axis=AX.X, op=ALU.add)
             nc.vector.reciprocal(out=rec[:], in_=tot[:])
             nc.vector.scalar_tensor_tensor(
-                out=sc[:], in0=f[:], scalar=post, in1=rec[:].unsqueeze(2).to_broadcast([P, 2, NCH]),
+                out=sc[:], in0=f[:], scalar=post, in1=rec[:].unsqueeze(2).to_broadcast([P, 2, n]),
                 op0=ALU.mult, op1=ALU.mult,
             )
             return sc
@@ -178,63 +207,92 @@ def tile_waveletmultiheadattention_w_kernel(
             cols = slice(c * CW, (c + 1) * CW)
             for g in range(G):
                 mx_pass(qk[c], g, wk[c][:, g, :], planes[1], cols, False, g == G - 1)
-            haar(qk[c], cb[0][c], t1[c])
-            shift_and_exp(t1[c], nm1, ss1, e1[c][:, 0, :], e1[c][:, 1, :], c)
+            haar_odd(qk[c], cb[0][c], t1[c])
+            haar_even(qk[c], t1[c])
+            maxes(t1[c], nm1, c)
+            exps(t1[c], nm1, ss1, e1[c][:, 0, :], e1[c][:, 1, :], c)
 
-        nm2 = keep.tile([P, 2, NCH], F32, name="nm2")
-        ss2 = keep.tile([P, 2, NCH], F32, name="ss2")
-        t2 = [keep.tile([P, 2, HW], F32, name="t2_%d" % c) for c in range(NCH)]
-        e2 = [keep.tile([P, 3, HW], F32, name="e2_%d" % c) for c in range(NCH)]
-        lb = [keep.tile([P, 2, HW], F32, name="lb%d" % c) for c in range(NCH)]
-        f1 = chunk_factors(nm1, "1")
-        sc1 = None
-        for c in range(NCH):
-            cols = slice(c * CW, (c + 1) * CW)
-            vb = psum.tile([P, CW], F32, name="v%d" % c, tag="b%d" % (4 + c))
+        nm2 = keep.tile([P, 2, NV], F32, name="nm2")
+        ss2 = keep.tile([P, 2, NV], F32, name="ss2")
+        t2 = [keep.tile([P, 2, VCH[i][1] // 2], F32, name="t2_%d" % i) for i in range(NV)]
+        e2 = [keep.tile([P, 3, VCH[i][1] // 2], F32, name="e2_%d" % i) for i in range(NV)]
+        lb = [keep.tile([P, 2, VCH[i][1] // 2], F32, name="lb%d" % i) for i in range(NV)]
+        f1 = chunk_factors(nm1, "1", NCH)
+        vb = [psum.tile([P, VCH[i][1]], F32, name="v%d" % i, tag="b%d" % VBANK[i]) for i in range(NV)]
+        for i, (c0, cw) in enumerate(VCH):
+            cols = slice(c0, c0 + cw)
             for g in range(G):
-                mx_pass(vb, g, wv[c][:, g, :], planes[2], cols, g == 0, g == G - 1)
-            if c == 0:
-                haar(vb, cb[1][0], t2[0])
-                sc1 = chunk_scales(f1, ss1, 1.0, "1")
-                for cc in (2, 3):
-                    for h in range(2):
-                        nc.scalar.activation(
-                            out=e1[cc][:, h, :], in_=e1[cc][:, h, :], func=ACT.Copy, scale=sc1[:, h, cc : cc + 1]
-                        )
-                    nc.gpsimd.tensor_tensor(out=lb[cc][:], in0=e1[cc][:], in1=cb[1][cc][:], op=ALU.add)
+                mx_pass(vb[i], g, wv[i][:, g, :], planes[2], cols, g == 0, g == G - 1)
+
+        def part(tiles, i):
+            c0, cw = VCH[i]
+            j0 = (c0 % CW) // 2
+            return tiles[c0 // CW][:, :, j0 : j0 + cw // 2]
+
+        if COMB_AFTER_ODD:
+            haar_odd(vb[0], part(cb[1], 0), t2[0])
+        sc1 = chunk_scales(f1, ss1, 1.0, "1", NCH)
+        for i in ACT_LS_ORDER:
+            qc = VCH[i][0] // CW
+            for h in range(2):
+                nc.scalar.activation(
+                    out=part(e1, i)[:, h, :], in_=part(e1, i)[:, h, :], func=ACT.Copy, scale=sc1[:, h, qc : qc + 1]
+                )
+        for i in range(NV):
+            if i in POST:
+                if not (i == 0 and COMB_AFTER_ODD):
+                    haar_odd(vb[i], part(cb[1], i), t2[i])
+                haar_even(vb[i], t2[i])
+                maxes(t2[i], nm2, i)
+        for i in POOL_ORDER:
+            if i in POST:
+                nc.gpsimd.tensor_tensor(out=t2[i][:], in0=t2[i][:], in1=part(e1, i), op=ALU.add)
+            else:
+                nc.gpsimd.tensor_tensor(out=lb[i][:], in0=part(e1, i), in1=part(cb[1], i), op=ALU.add)
+        for i in range(NV):
+            if i in POST:
+                continue
+            if i in DVE_LB:
+                qc = VCH[i][0] // CW
                 for h in range(2):
                     nc.vector.scalar_tensor_tensor(
-                        out=t2[0][:, h, :], in0=e1[0][:, h, :], scalar=sc1[:, h, 0:1], in1=t2[0][:, h, :],
-                        op0=ALU.mult, op1=ALU.add,
+                        out=lb[i][:, h, :], in0=part(e1, i)[:, h, :], scalar=sc1[:, h, qc : qc + 1],
+                        in1=part(cb[1], i)[:, h, :], op0=ALU.mult, op1=ALU.add,
                     )
+            haar_odd(vb[i], lb[i], t2[i])
+            haar_even(vb[i], t2[i])
+            maxes(t2[i], nm2, i)
+
+        def negate(i):
+            if i in NEG_ON_ACT:
+                nc.scalar.activation(out=e2[i][:, 1, :], in_=e2[i][:, 2, :], func=ACT.Copy, scale=-1.0)
             else:
-                if c == 1:
-                    for h in range(2):
-                        nc.vector.scalar_tensor_tensor(
-                            out=lb[1][:, h, :], in0=e1[1][:, h, :], scalar=sc1[:, h, 1:2], in1=cb[1][1][:, h, :],
-                            op0=ALU.mult, op1=ALU.add,
-                        )
-                haar(vb, lb[c], t2[c])
-            shift_and_exp(t2[c], nm2, ss2, e2[c][:, 0, :], e2[c][:, 2, :], c)
-            nc.gpsimd.tensor_scalar(
-                out=e2[c][:, 1, :], in0=e2[c][:, 2, :], scalar1=-1.0, scalar2=0.0, op0=ALU.mult, op1=ALU.add
-            )
-        sc2 = chunk_scales(chunk_factors(nm2, "2"), ss2, C, "2")
+                nc.gpsimd.tensor_scalar(
+                    out=e2[i][:, 1, :], in0=e2[i][:, 2, :], scalar1=-1.0, scalar2=0.0, op0=ALU.mult, op1=ALU.add
+                )
+
+        for i in EXP_ORDER:
+            exps(t2[i], nm2, ss2, e2[i][:, 0, :], e2[i][:, 2, :], i)
+            if i != EXP_ORDER[-1]:
+                negate(i)
+        f2 = chunk_factors(nm2, "2", NV)
+        negate(EXP_ORDER[-1])
+        sc2 = chunk_scales(f2, ss2, C, "2", NV)
         out2d = out.flatten_outer_dims()
-        for c in range(NCH):
-            low = keep.tile([P, HW], F32, name="low%d" % c)
-            res = keep.tile([P, CW], F32, name="res%d" % c)
-            if c == 0:
+        for i, (c0, cw) in enumerate(VCH):
+            low = keep.tile([P, cw // 2], F32, name="low%d" % i)
+            res = keep.tile([P, cw], F32, name="res%d" % i)
+            if i == 0:
                 nc.vector.tensor_scalar(
-                    out=low[:], in0=e2[c][:, 0, :], scalar1=sc2[:, 0, c : c + 1], scalar2=None, op0=ALU.mult
+                    out=low[:], in0=e2[i][:, 0, :], scalar1=sc2[:, 0, i : i + 1], scalar2=None, op0=ALU.mult
                 )
             else:
-                nc.scalar.activation(out=low[:], in_=e2[c][:, 0, :], func=ACT.Copy, scale=sc2[:, 0, c : c + 1])
+                nc.scalar.activation(out=low[:], in_=e2[i][:, 0, :], func=ACT.Copy, scale=sc2[:, 0, i : i + 1])
             nc.vector.scalar_tensor_tensor(
                 out=res[:].rearrange("p (j t) -> p j t", t=2),
-                in0=e2[c][:, 1:3, :].rearrange("p t j -> p j t"),
-                scalar=sc2[:, 1, c : c + 1],
-                in1=low[:].unsqueeze(2).to_broadcast([P, HW, 2]),
+                in0=e2[i][:, 1:3, :].rearrange("p t j -> p j t"),
+                scalar=sc2[:, 1, i : i + 1],
+                in1=low[:].unsqueeze(2).to_broadcast([P, cw // 2, 2]),
                 op0=ALU.mult, op1=ALU.add,
             )
-            nc.sync.dma_start(out=out2d[:, c * CW : (c + 1) * CW], in_=res[:])
+            nc.sync.dma_start(out=out2d[:, c0 : c0 + cw], in_=res[:])

@@ -23,11 +23,11 @@ CW = 512
 HW = 256
 C = 0.7071067811865476
 
-SPLIT_K = (3,)
+SPLIT_K = (0, 1, 2, 3)
 VCH = ((0, 512), (512, 512), (1024, 512), (1536, 512))
 NV = len(VCH)
 VBANK = (4, 5, 6, 7)
-SPLIT_V = (0, 3)
+SPLIT_V = (0, 1, 2, 3)
 POST = (0, 1)
 POOL_ORDER = (2, 3, 0, 1)
 ACT_LS_ORDER = (2, 3, 0, 1)

@@ -33,7 +33,7 @@ POOL_ORDER = (2, 3, 0, 1)
 ACT_LS_ORDER = (2, 3, 0, 1)
 EXP_ORDER = (0, 2, 1, 3)
 COMB_AFTER_ODD = True
-NEG_ON_ACT = (3,)
+NEG_ON_ACT = (1, 3)
 VSCALES_LATE = True
 DVE_LB = ()
 
@@ -149,12 +149,15 @@ def tile_waveletmultiheadattention_w_kernel(
                     out=t[:, h, :], in0=odd, scalar=C, in1=addend[:, h, :], op0=ALU.mult, op1=ALU.add
                 )
 
-        def haar_even(bank, t):
+        def haar_even_half(bank, t, h):
             even = bank[:].rearrange("p (j t) -> p j t", t=2)[:, :, 0]
+            nc.vector.scalar_tensor_tensor(
+                out=t[:, h, :], in0=even, scalar=(C, -C)[h], in1=t[:, h, :], op0=ALU.mult, op1=ALU.add
+            )
+
+        def haar_even(bank, t):
             for h in range(2):
-                nc.vector.scalar_tensor_tensor(
-                    out=t[:, h, :], in0=even, scalar=(C, -C)[h], in1=t[:, h, :], op0=ALU.mult, op1=ALU.add
-                )
+                haar_even_half(bank, t, h)
 
         def maxes(t, nm, c):
             for h in range(2):
@@ -180,19 +183,29 @@ def tile_waveletmultiheadattention_w_kernel(
                 )
             return f
 
-        def chunk_scales(f, ss, post, tag, n):
+        def chunk_scale_steps(f, ss, post, tag, n):
             fs = keep.tile([P, 2, n], F32, name="fs" + tag)
             tot = keep.tile([P, 2], F32, name="tot" + tag)
             rec = keep.tile([P, 2], F32, name="rec" + tag)
             sc = keep.tile([P, 2, n], F32, name="sc" + tag)
-            nc.vector.tensor_tensor(out=fs[:], in0=f[:], in1=ss[:], op=ALU.mult)
-            nc.vector.tensor_reduce(out=tot[:], in_=fs[:], axis=AX.X, op=ALU.add)
-            nc.vector.reciprocal(out=rec[:], in_=tot[:])
-            nc.vector.scalar_tensor_tensor(
-                out=sc[:], in0=f[:], scalar=post, in1=rec[:].unsqueeze(2).to_broadcast([P, 2, n]),
-                op0=ALU.mult, op1=ALU.mult,
-            )
-            return sc
+
+            def total(h):
+                nc.vector.scalar_tensor_tensor(
+                    out=fs[:, h, :], in0=f[:, h, :], scalar=1.0, in1=ss[:, h, :], op0=ALU.mult, op1=ALU.mult,
+                    accum_out=tot[:, h : h + 1],
+                )
+
+            def inverse(h0, h1):
+                nc.vector.reciprocal(out=rec[:, h0:h1], in_=tot[:, h0:h1])
+
+            def scale(h0, h1):
+                nc.vector.scalar_tensor_tensor(
+                    out=sc[:, h0:h1, :], in0=f[:, h0:h1, :], scalar=post,
+                    in1=rec[:, h0:h1].unsqueeze(2).to_broadcast([P, h1 - h0, n]),
+                    op0=ALU.mult, op1=ALU.mult,
+                )
+
+            return sc, total, inverse, scale
 
         qk = [psum.tile([P, CW], F32, name="qk%d" % c, tag="b%d" % c) for c in range(NCH)]
         for g in range(G):
@@ -229,9 +242,15 @@ def tile_waveletmultiheadattention_w_kernel(
             j0 = (c0 % CW) // 2
             return tiles[c0 // CW][:, :, j0 : j0 + cw // 2]
 
-        if COMB_AFTER_ODD:
-            haar_odd(vb[0], part(cb[1], 0), t2[0])
-        sc1 = chunk_scales(f1, ss1, 1.0, "1", NCH)
+        haar_odd(vb[0], part(cb[1], 0), t2[0])
+        sc1, total1, inverse1, scale1 = chunk_scale_steps(f1, ss1, 1.0, "1", NCH)
+        total1(0)
+        total1(1)
+        haar_even_half(vb[0], t2[0], 0)
+        inverse1(0, 2)
+        haar_even_half(vb[0], t2[0], 1)
+        scale1(0, 2)
+        maxes(t2[0], nm2, 0)
         for i in ACT_LS_ORDER:
             qc = VCH[i][0] // CW
             for h in range(2):
@@ -240,8 +259,9 @@ def tile_waveletmultiheadattention_w_kernel(
                 )
         for i in range(NV):
             if i in POST:
-                if not (i == 0 and COMB_AFTER_ODD):
-                    haar_odd(vb[i], part(cb[1], i), t2[i])
+                if i == 0:
+                    continue
+                haar_odd(vb[i], part(cb[1], i), t2[i])
                 haar_even(vb[i], t2[i])
                 maxes(t2[i], nm2, i)
         for i in POOL_ORDER:
@@ -273,11 +293,18 @@ def tile_waveletmultiheadattention_w_kernel(
 
         for i in EXP_ORDER:
             exps(t2[i], nm2, ss2, e2[i][:, 0, :], e2[i][:, 2, :], i)
-            if i != EXP_ORDER[-1]:
+            if i not in NEG_ON_ACT:
                 negate(i)
         f2 = chunk_factors(nm2, "2", NV)
-        negate(EXP_ORDER[-1])
-        sc2 = chunk_scales(f2, ss2, C, "2", NV)
+        for i in NEG_ON_ACT:
+            negate(i)
+        sc2, total2, inverse2, scale2 = chunk_scale_steps(f2, ss2, C, "2", NV)
+        for h in range(2):
+            total2(h)
+        for h in range(2):
+            inverse2(h, h + 1)
+        for h in range(2):
+            scale2(h, h + 1)
         out2d = out.flatten_outer_dims()
         for i, (c0, cw) in enumerate(VCH):
             low = keep.tile([P, cw // 2], F32, name="low%d" % i)

@@ -71,7 +71,7 @@ def tile_waveletmultiheadattention_w_kernel(
         nc.scalar.dma_start(out=rows[1:2, 0, :], in_=b_k.unsqueeze(0))
         nc.scalar.dma_start(out=rows[0:1, 1, :], in_=b_v.unsqueeze(0))
         def load_scales(w, sc):
-            for q in range(4):
+            for q in (0, 2, 1, 3):
                 nc.sync.dma_start(
                     out=planes[w][32 * q : 32 * q + 16, :].bitcast(I32),
                     in_=sc[:, 4 * q : 4 * q + 4, :].bitcast(I32),

from contextlib import ExitStack

import concourse.masks as masks
import concourse.mybir as mybir

FLOPS = 3 * 2 * 128 * 2048 * 2048

F32 = mybir.dt.float32
BF16 = mybir.dt.bfloat16
U8 = mybir.dt.uint8
U32 = mybir.dt.uint32
I32 = mybir.dt.int32
FP8X4 = mybir.dt.float8_e4m3fn_x4
ALU = mybir.AluOpType
ACT = mybir.ActivationFunctionType
AX = mybir.AxisListType

P = 128
D = 2048
G = 4
NCH = 4
CW = 512
HW = 256
C = 0.7071067811865476

SPLIT_K = (0, 1, 2, 3)
VCH = ((0, 512), (512, 512), (1024, 512), (1536, 512))
NV = len(VCH)
VBANK = (4, 5, 6, 7)
SPLIT_V = (0, 1, 2, 3)
POST = (0, 1)
POOL_ORDER = (2, 3, 0, 1)
ACT_LS_ORDER = (2, 3, 0, 1)
EXP_ORDER = (0, 2, 1, 3)
COMB_AFTER_ODD = True
NEG_ON_ACT = (1, 3)
VSCALES_LATE = True
DVE_LB = ()


def tile_waveletmultiheadattention_w_kernel(
    tc, x, wq_words, wq_scales, b_q, wk_words, wk_scales, b_k, wv_words, wv_scales, b_v, out
):
    nc = tc.nc
    with ExitStack() as ctx:
        keep = ctx.enter_context(tc.tile_pool(name="keep", bufs=1))
        psum = ctx.enter_context(tc.psum_pool(name="psum", bufs=1))
        ctx.enter_context(tc.manual_schedule())

        zero1 = keep.tile([P, 1], F32, name="zero1")
        warm = keep.tile([P, 1], F32, name="warm")
        nc.vector.memset(zero1[:], 0.0)
        nc.scalar.activation(out=warm[:], in_=zero1[:], func=ACT.Exp)

        planes = [keep.tile([P, D], U8, name="planes%d" % w, align_bytes=64) for w in range(3)]
        for w in range(3):
            nc.vector.memset(planes[w][:].bitcast(I32), 0)
        rows = keep.tile([P, 2, D], BF16, name="rows")
        nc.vector.memset(rows[:].rearrange("p w n -> p (w n)").bitcast(I32), 0)

        ident = keep.tile([P, P], F32, name="ident")
        masks.make_identity(nc, ident[:])
        pos = keep.tile([P, P], BF16, name="pos")
        neg = keep.tile([P, P], BF16, name="neg")
        nc.gpsimd.memset(pos[:], 1.0)
        nc.gpsimd.memset(neg[:], -1.0)

        x_sb = keep.tile([P, D], BF16, name="x_sb")
        nc.sync.dma_start(out=x_sb[:], in_=x.flatten_outer_dims())
        nc.scalar.dma_start(out=rows[0:1, 0, :], in_=b_q.unsqueeze(0))
        nc.scalar.dma_start(out=rows[1:2, 0, :], in_=b_k.unsqueeze(0))
        nc.scalar.dma_start(out=rows[0:1, 1, :], in_=b_v.unsqueeze(0))
        def load_scales(w, sc):
            for q in (0, 2, 1, 3):
                nc.sync.dma_start(
                    out=planes[w][32 * q : 32 * q + 16, :].bitcast(I32),
                    in_=sc[:, 4 * q : 4 * q + 4, :].bitcast(I32),
                )

        load_scales(0, wq_scales)
        load_scales(1, wk_scales)
        if not VSCALES_LATE:
            load_scales(2, wv_scales)
        wq = [keep.tile([P, D], U32, name="wq%d" % g, align_bytes=64) for g in range(G)]
        for g in range(G):
            nc.sync.dma_start(
                out=wq[g][:].bitcast(I32),
                in_=wq_words[g].rearrange("p n t -> p (n t)").bitcast(I32),
            )
        wk = [keep.tile([P, G, CW], U32, name="wk%d" % c, align_bytes=64) for c in range(NCH)]
        wv = [keep.tile([P, G, VCH[i][1]], U32, name="wv%d" % i, align_bytes=64) for i in range(NV)]
        KCH = tuple((c * CW, CW) for c in range(NCH))
        for tiles, words, split, chunks in ((wk, wk_words, SPLIT_K, KCH), (wv, wv_words, SPLIT_V, VCH)):
            view = words.rearrange("g p n t -> p g (n t)").bitcast(I32)
            if VSCALES_LATE and tiles is wv:
                load_scales(2, wv_scales)
            for c, (c0, cw) in enumerate(chunks):
                cols = slice(c0, c0 + cw)
                if c in split:
                    nc.sync.dma_start(out=tiles[c][:, 0:3, :].bitcast(I32), in_=view[:, 0:3, cols])
                    nc.sync.dma_start(out=tiles[c][:, 3:4, :].bitcast(I32), in_=view[:, 3:4, cols])
                else:
                    nc.sync.dma_start(out=tiles[c][:].bitcast(I32), in_=view[:, :, cols])

        x32 = x_sb[:].bitcast(F32)
        grouped = keep.tile([P, D], BF16, name="grouped", align_bytes=64)
        g32 = grouped[:].bitcast(F32).rearrange("p (g r u) -> p g r u", g=G, u=2)
        xt = [psum.tile([P, 2, 2, P], F32, name="xt%d" % b, tag="b%d" % (4 + b)) for b in range(2)]
        for g in range(G):
            for u in range(2):
                nc.tensor.transpose(
                    out=xt[g // 2][:, g % 2, u, :],
                    in_=x32[:, 256 * g + u : 256 * (g + 1) : 2],
                    identity=ident[:],
                )
        nc.vector.tensor_copy(out=g32[:, 0:2], in_=xt[0][:].rearrange("p g u r -> p g r u"))
        nc.scalar.copy(out=g32[:, 2:4], in_=xt[1][:].rearrange("p g u r -> p g r u"))
        xc = keep.tile([P, G * P], U32, name="xc", align_bytes=64)
        xs = keep.tile([P, G * P], U8, name="xs", align_bytes=64)
        nc.vector.quantize_mx(out=xc[:].bitcast(FP8X4), scales=xs[:], in_=grouped[:])

        cb = [[keep.tile([P, 2, HW], F32, name="cb%d_%d" % (w, c)) for c in range(NCH)] for w in range(2)]
        bias_banks = (6, 7, 4, 5)
        for w in range(2):
            rv = rows[:, w, :].rearrange("p (c j t) -> p c j t", c=NCH, t=2)
            for c in range(NCH):
                bb = psum.tile([P, 2, HW], F32, name="bb%d_%d" % (w, c), tag="b%d" % bias_banks[c])
                nc.tensor.matmul(out=bb[:, 0, :], lhsT=pos[:], rhs=rv[:, c, :, 0], start=True, stop=False)
                nc.tensor.matmul(out=bb[:, 0, :], lhsT=pos[:], rhs=rv[:, c, :, 1], start=False, stop=True)
                nc.tensor.matmul(out=bb[:, 1, :], lhsT=pos[:], rhs=rv[:, c, :, 1], start=True, stop=False)
                nc.tensor.matmul(out=bb[:, 1, :], lhsT=neg[:], rhs=rv[:, c, :, 0], start=False, stop=True)
                nc.scalar.activation(out=cb[w][c][:], in_=bb[:], func=ACT.Copy, scale=C)

        def mx_pass(bank, g, words, plane, cols, start, stop):
            nc.tensor.matmul_mx(
                out=bank[:],
                lhsT=xc[:, g * P : (g + 1) * P].bitcast(FP8X4),
                lhsT_scale=xs[:, g * P : (g + 1) * P],
                rhs=words.bitcast(FP8X4),
                rhs_scale=plane[4 * g : P, cols],
                start=start,
                stop=stop,
            )

        def haar_odd(bank, addend, t):
            odd = bank[:].rearrange("p (j t) -> p j t", t=2)[:, :, 1]
            for h in range(2):
                nc.vector.scalar_tensor_tensor(
                    out=t[:, h, :], in0=odd, scalar=C, in1=addend[:, h, :], op0=ALU.mult, op1=ALU.add
                )

        def haar_even_half(bank, t, h):
            even = bank[:].rearrange("p (j t) -> p j t", t=2)[:, :, 0]
            nc.vector.scalar_tensor_tensor(
                out=t[:, h, :], in0=even, scalar=(C, -C)[h], in1=t[:, h, :], op0=ALU.mult, op1=ALU.add
            )

        def haar_even(bank, t):
            for h in range(2):
                haar_even_half(bank, t, h)

        def maxes(t, nm, c):
            for h in range(2):
                nc.vector.tensor_reduce(out=nm[:, h, c : c + 1], in_=t[:, h, :], axis=AX.X, op=ALU.max, negate=True)

        def exps(t, nm, ss, e_low, e_high, c):
            nc.scalar.activation(
                out=e_low, in_=t[:, 0, :], func=ACT.Exp, bias=nm[:, 0, c : c + 1], scale=1.0,
                accum_out=ss[:, 0, c : c + 1],
            )
            nc.scalar.activation(
                out=e_high, in_=t[:, 1, :], func=ACT.Exp, bias=nm[:, 1, c : c + 1], scale=1.0,
                accum_out=ss[:, 1, c : c + 1],
            )

        def chunk_factors(nm, tag, n):
            gm = keep.tile([P, 2], F32, name="gm" + tag)
            f = keep.tile([P, 2, n], F32, name="f" + tag)
            nc.vector.tensor_reduce(out=gm[:], in_=nm[:], axis=AX.X, op=ALU.min)
            for h in range(2):
                nc.scalar.activation(
                    out=f[:, h, :], in_=nm[:, h, :], func=ACT.Exp, bias=gm[:, h : h + 1], scale=-1.0
                )
            return f

        def chunk_scale_steps(f, ss, post, tag, n):
            fs = keep.tile([P, 2, n], F32, name="fs" + tag)
            tot = keep.tile([P, 2], F32, name="tot" + tag)
            rec = keep.tile([P, 2], F32, name="rec" + tag)
            sc = keep.tile([P, 2, n], F32, name="sc" + tag)

            def total(h):
                nc.vector.scalar_tensor_tensor(
                    out=fs[:, h, :], in0=f[:, h, :], scalar=1.0, in1=ss[:, h, :], op0=ALU.mult, op1=ALU.mult,
                    accum_out=tot[:, h : h + 1],
                )

            def inverse(h0, h1):
                nc.vector.reciprocal(out=rec[:, h0:h1], in_=tot[:, h0:h1])

            def scale(h0, h1):
                nc.vector.scalar_tensor_tensor(
                    out=sc[:, h0:h1, :], in0=f[:, h0:h1, :], scalar=post,
                    in1=rec[:, h0:h1].unsqueeze(2).to_broadcast([P, h1 - h0, n]),
                    op0=ALU.mult, op1=ALU.mult,
                )

            return sc, total, inverse, scale

        qk = [psum.tile([P, CW], F32, name="qk%d" % c, tag="b%d" % c) for c in range(NCH)]
        for g in range(G):
            for c in range(NCH):
                cols = slice(c * CW, (c + 1) * CW)
                mx_pass(qk[c], g, wq[g][:, cols], planes[0], cols, g == 0, False)
        nm1 = keep.tile([P, 2, NCH], F32, name="nm1")
        ss1 = keep.tile([P, 2, NCH], F32, name="ss1")
        t1 = [keep.tile([P, 2, HW], F32, name="t1_%d" % c) for c in range(NCH)]
        e1 = [keep.tile([P, 2, HW], F32, name="e1_%d" % c) for c in range(NCH)]
        for c in range(NCH):
            cols = slice(c * CW, (c + 1) * CW)
            for g in range(G):
                mx_pass(qk[c], g, wk[c][:, g, :], planes[1], cols, False, g == G - 1)
            haar_odd(qk[c], cb[0][c], t1[c])
            haar_even(qk[c], t1[c])
            maxes(t1[c], nm1, c)
            exps(t1[c], nm1, ss1, e1[c][:, 0, :], e1[c][:, 1, :], c)

        nm2 = keep.tile([P, 2, NV], F32, name="nm2")
        ss2 = keep.tile([P, 2, NV], F32, name="ss2")
        t2 = [keep.tile([P, 2, VCH[i][1] // 2], F32, name="t2_%d" % i) for i in range(NV)]
        e2 = [keep.tile([P, 3, VCH[i][1] // 2], F32, name="e2_%d" % i) for i in range(NV)]
        lb = [keep.tile([P, 2, VCH[i][1] // 2], F32, name="lb%d" % i) for i in range(NV)]
        f1 = chunk_factors(nm1, "1", NCH)
        vb = [psum.tile([P, VCH[i][1]], F32, name="v%d" % i, tag="b%d" % VBANK[i]) for i in range(NV)]
        for i, (c0, cw) in enumerate(VCH):
            cols = slice(c0, c0 + cw)
            for g in range(G):
                mx_pass(vb[i], g, wv[i][:, g, :], planes[2], cols, g == 0, g == G - 1)

        def part(tiles, i):
            c0, cw = VCH[i]
            j0 = (c0 % CW) // 2
            return tiles[c0 // CW][:, :, j0 : j0 + cw // 2]

        haar_odd(vb[0], part(cb[1], 0), t2[0])
        sc1, total1, inverse1, scale1 = chunk_scale_steps(f1, ss1, 1.0, "1", NCH)
        total1(0)
        total1(1)
        haar_even_half(vb[0], t2[0], 0)
        inverse1(0, 2)
        haar_even_half(vb[0], t2[0], 1)
        scale1(0, 2)
        maxes(t2[0], nm2, 0)
        for i in ACT_LS_ORDER:
            qc = VCH[i][0] // CW
            for h in range(2):
                nc.scalar.activation(
                    out=part(e1, i)[:, h, :], in_=part(e1, i)[:, h, :], func=ACT.Copy, scale=sc1[:, h, qc : qc + 1]
                )
        for i in range(NV):
            if i in POST:
                if i == 0:
                    continue
                haar_odd(vb[i], part(cb[1], i), t2[i])
                haar_even(vb[i], t2[i])
                maxes(t2[i], nm2, i)
        for i in POOL_ORDER:
            if i in POST:
                nc.gpsimd.tensor_tensor(out=t2[i][:], in0=t2[i][:], in1=part(e1, i), op=ALU.add)
            else:
                nc.gpsimd.tensor_tensor(out=lb[i][:], in0=part(e1, i), in1=part(cb[1], i), op=ALU.add)
        for i in range(NV):
            if i in POST:
                continue
            if i in DVE_LB:
                qc = VCH[i][0] // CW
                for h in range(2):
                    nc.vector.scalar_tensor_tensor(
                        out=lb[i][:, h, :], in0=part(e1, i)[:, h, :], scalar=sc1[:, h, qc : qc + 1],
                        in1=part(cb[1], i)[:, h, :], op0=ALU.mult, op1=ALU.add,
                    )
            haar_odd(vb[i], lb[i], t2[i])
            haar_even(vb[i], t2[i])
            maxes(t2[i], nm2, i)

        def negate(i):
            if i in NEG_ON_ACT:
                nc.scalar.activation(out=e2[i][:, 1, :], in_=e2[i][:, 2, :], func=ACT.Copy, scale=-1.0)
            else:
                nc.gpsimd.tensor_scalar(
                    out=e2[i][:, 1, :], in0=e2[i][:, 2, :], scalar1=-1.0, scalar2=0.0, op0=ALU.mult, op1=ALU.add
                )

        for i in EXP_ORDER:
            exps(t2[i], nm2, ss2, e2[i][:, 0, :], e2[i][:, 2, :], i)
            if i not in NEG_ON_ACT:
                negate(i)
        f2 = chunk_factors(nm2, "2", NV)
        for i in NEG_ON_ACT:
            negate(i)
        sc2, total2, inverse2, scale2 = chunk_scale_steps(f2, ss2, C, "2", NV)
        for h in range(2):
            total2(h)
        for h in range(2):
            inverse2(h, h + 1)
        for h in range(2):
            scale2(h, h + 1)
        out2d = out.flatten_outer_dims()
        for i, (c0, cw) in enumerate(VCH):
            low = keep.tile([P, cw // 2], F32, name="low%d" % i)
            res = keep.tile([P, cw], F32, name="res%d" % i)
            if i == 0:
                nc.vector.tensor_scalar(
                    out=low[:], in0=e2[i][:, 0, :], scalar1=sc2[:, 0, i : i + 1], scalar2=None, op0=ALU.mult
                )
            else:
                nc.scalar.activation(out=low[:], in_=e2[i][:, 0, :], func=ACT.Copy, scale=sc2[:, 0, i : i + 1])
            nc.vector.scalar_tensor_tensor(
                out=res[:].rearrange("p (j t) -> p j t", t=2),
                in0=e2[i][:, 1:3, :].rearrange("p t j -> p j t"),
                scalar=sc2[:, 1, i : i + 1],
                in1=low[:].unsqueeze(2).to_broadcast([P, cw // 2, 2]),
                op0=ALU.mult, op1=ALU.add,
            )
            nc.sync.dma_start(out=out2d[:, c0 : c0 + cw], in_=res[:])
